import numpy as np
import ml_dtypes


def mxq(x, axis, fmt="e4m3"):
    dtype, down = {"e4m3": (ml_dtypes.float8_e4m3fn, 7), "e5m2": (ml_dtypes.float8_e5m2, 14)}[fmt]
    v = np.moveaxis(np.asarray(x, np.float32).astype(ml_dtypes.bfloat16).astype(np.float64), axis, -1)
    blocks = v.reshape(v.shape[:-1] + (-1, 32))
    amax = np.abs(blocks).max(-1, keepdims=True)
    byte = np.maximum(np.where(amax > 0, np.frexp(amax)[1] - 1 + 127, 0) - down, 1)
    scale = np.exp2(byte - 127.0)
    codes = (blocks / scale).astype(np.float32).astype(dtype).astype(np.float64)
    return np.moveaxis((codes * scale).reshape(v.shape), -1, axis)


WIDE = False


def mx_kscale(k):
    if not WIDE:
        return np.ones(k)
    levels = np.array([10, -10, 5, -5, 0])
    a = np.random.permutation(np.resize(levels, k // 512 * 4)).reshape(k // 512, 4)
    idx = np.arange(k)
    return np.exp2(a[idx // 512, idx % 128 // 32])


BF16 = ml_dtypes.bfloat16


def bf(x):
    return np.asarray(x, np.float32).astype(BF16)


def f64(x):
    return np.asarray(x).astype(np.float64)


S, A, B, K, H, G = 32, 8, 16, 512, 256, 3


def sigmoid(v):
    return 1.0 / (1.0 + np.exp(-v))


def setup_inputs():
    s = mx_kscale(K)
    c = 0.7 / np.sqrt(K)
    return {"x": bf(np.random.standard_normal((S + 1, A, B, K)) * s),
            "x_mix": bf(np.random.standard_normal((S + 1, A, B, H))),
            "WL": bf(np.random.standard_normal((H, K)) * c / s),
            "WR": bf(np.random.standard_normal((H, K)) * c / s),
            "GL": bf(np.random.standard_normal((G * H, K)) * c / s),
            "GR": bf(np.random.standard_normal((G * H, K)) * c / s)}


def reference(x, x_mix, WL, WR, GL, GR):
    xm = f64(x_mix)
    left, right = xm[:-1], xm[1:]
    xq = mxq(f64(x), 3, "e4m3")
    lq, rq = xq[:-1], xq[1:]
    center = sigmoid((lq @ mxq(f64(WL), 1, "e4m3").T) + (rq @ mxq(f64(WR), 1, "e4m3").T))
    gate = (lq @ mxq(f64(GL), 1, "e4m3").T) + (rq @ mxq(f64(GR), 1, "e4m3").T)
    g = gate.reshape(gate.shape[:-1] + (G, H))
    e = np.exp(g - g.max(-2, keepdims=True))
    w = e / e.sum(-2, keepdims=True)
    return left * w[..., 0, :] + right * w[..., 1, :] + center * w[..., 2, :]

@@ -1,0 +1,278 @@
+from contextlib import ExitStack
+
+import concourse.mybir as mybir
+from concourse.masks import make_identity
+
+F32 = mybir.dt.float32
+BF16 = mybir.dt.bfloat16
+U32 = mybir.dt.uint32
+U8 = mybir.dt.uint8
+FP8X4 = mybir.dt.float8_e4m3fn_x4
+AF = mybir.ActivationFunctionType
+ALU = mybir.AluOpType
+
+P = 128
+K = 512
+H = 256
+POSITIONS = 32
+BLOCKS = POSITIONS + 1
+PAIRS = POSITIONS // 2
+PAIR_COLS = 2 * H
+UNITS = (BLOCKS + 1) // 2
+ROUND = 8
+LOAD_BLOCKS = 4
+
+LEFT, RIGHT = 0, 1
+OPERANDS = ("centre", "g0", "g1", "neg_g1", "neg_g2")
+CHUNK_USES = {"centre": ("centre", None), "g0": ("g0", None), "g1": ("g1", "neg_g1"), "g2": (None, "neg_g2")}
+GATE_CHUNK = {"g0": 0, "g1": 1, "g2": 2}
+
+FLOPS = 2 * POSITIONS * P * (2 * K) * (4 * H)
+
+
+def tile_grconv_pa_t_kernel(tc, x, x_mix, WL, WR, GL, GR, out):
+    nc = tc.nc
+    x_rows = x.rearrange("s a b k -> (a b) s k")
+    mix_rows = x_mix.rearrange("s a b h -> (a b) s h")
+    out_rows = out.rearrange("s a b h -> (a b) s h")
+    centres = (WL, WR)
+    gates = (GL, GR)
+
+    with ExitStack() as ctx:
+        ctx.enter_context(tc.manual_schedule())
+        const = ctx.enter_context(tc.tile_pool(name="const", bufs=1))
+        resident = ctx.enter_context(tc.tile_pool(name="resident", bufs=1))
+        stage = ctx.enter_context(tc.tile_pool(name="stage", bufs=3))
+        keep = ctx.enter_context(tc.tile_pool(name="keep", bufs=ROUND + 1))
+        psum = ctx.enter_context(tc.psum_pool(name="psum", bufs=1))
+
+        plus_half = const.tile([P, 1], F32)
+        nc.vector.memset(plus_half[:], 0.5)
+        minus_half = const.tile([P, 1], F32)
+        nc.vector.memset(minus_half[:], -0.5)
+        warm = const.tile([P, 1], F32)
+        nc.scalar.activation(out=warm[:], in_=plus_half[:], func=AF.Sigmoid)
+        ident_words = const.tile([P, P], F32)
+        make_identity(nc, ident_words[:])
+        ident = const.tile([P, P], BF16)
+        make_identity(nc, ident[:])
+        neg_ident = const.tile([P, P], BF16)
+        nc.vector.tensor_scalar_mul(out=neg_ident[:], in0=ident[:], scalar1=-1.0)
+
+        x_nat = resident.tile([P, BLOCKS, K], BF16)
+        mix_in = resident.tile([P, BLOCKS, H], BF16)
+        x_codes = resident.tile([P, BLOCKS, P], U32, align_bytes=64)
+        x_scales = resident.tile([P, BLOCKS, P], U8, align_bytes=64)
+        w_codes = resident.tile([P, 2 * len(OPERANDS), H], U32, align_bytes=64)
+        w_scales = resident.tile([P, 2 * len(OPERANDS), H], U8, align_bytes=64)
+        w_nat = {}
+
+        def operand(side, name):
+            return side * len(OPERANDS) + OPERANDS.index(name)
+
+        def load_weight(side, chunk):
+            if chunk == "centre":
+                rows = centres[side]
+            else:
+                rows = gates[side][GATE_CHUNK[chunk] * H : (GATE_CHUNK[chunk] + 1) * H, :]
+            w_nat[(side, chunk)] = resident.tile([P, H // P, K], BF16, name="w_nat_%d_%s" % (side, chunk))
+            nc.sync.dma_start(out=w_nat[(side, chunk)][:], in_=rows.rearrange("(t p) k -> p t k", p=P))
+
+        def load_blocks(first):
+            last = min(first + LOAD_BLOCKS, BLOCKS)
+            nc.sync.dma_start(out=x_nat[:, first:last, :], in_=x_rows[:, first:last, :])
+            nc.sync.dma_start(out=mix_in[:, first:last, :], in_=mix_rows[:, first:last, :])
+
+        for side in (LEFT, RIGHT):
+            load_weight(side, "g0")
+            load_weight(side, "g1")
+        load_blocks(0)
+        for side in (LEFT, RIGHT):
+            load_weight(side, "centre")
+        load_blocks(LOAD_BLOCKS)
+        for side in (LEFT, RIGHT):
+            load_weight(side, "g2")
+        for first in range(2 * LOAD_BLOCKS, BLOCKS, LOAD_BLOCKS):
+            load_blocks(first)
+
+        def spread(nat, copy):
+            tiles = nat.shape[1]
+            rows = tiles * P
+            nat_words = nat.bitcast(F32)
+            words = psum.tile([P, 2, rows], F32, tag="words", bufs=2)
+            for u in range(2):
+                for t in range(tiles):
+                    nc.tensor.transpose(
+                        out=words[:, u, t * P : (t + 1) * P],
+                        in_=nat_words[:, t, u * P : (u + 1) * P],
+                        identity=ident_words[:],
+                    )
+            grouped = stage.tile([P, 4 * rows], BF16, tag="grouped", align_bytes=64)
+            copy(
+                out=grouped[:].bitcast(F32).rearrange("p (r u) -> p r u", u=2),
+                in_=words[:].rearrange("p u r -> p r u"),
+            )
+            return grouped
+
+        def quantise(values, codes, scales):
+            nc.vector.quantize_mx(out=codes.bitcast(FP8X4), scales=scales, in_=values)
+
+        def copy_engine(n):
+            return nc.scalar.copy if n % 2 == 0 else nc.vector.tensor_copy
+
+        def prepare_weight(side, chunk):
+            grouped = spread(w_nat[(side, chunk)][:], copy_engine(side))
+            plain, negated = CHUNK_USES[chunk]
+            if plain is not None:
+                w = operand(side, plain)
+                quantise(grouped[:], w_codes[:, w, :], w_scales[:, w, :])
+            if negated is not None:
+                w = operand(side, negated)
+                turned = stage.tile([P, 4 * H], BF16, tag="turned", align_bytes=64)
+                nc.vector.tensor_scalar_mul(out=turned[:], in0=grouped[:], scalar1=-1.0)
+                quantise(turned[:], w_codes[:, w, :], w_scales[:, w, :])
+
+        x_grouped = {}
+
+        def unit_blocks(unit):
+            return slice(2 * unit, min(2 * unit + 2, BLOCKS))
+
+        def spread_unit(unit):
+            x_grouped[unit] = spread(x_nat[:, unit_blocks(unit), :], copy_engine(unit))
+
+        def quantise_unit(unit):
+            quantise(
+                x_grouped[unit][:],
+                x_codes[:, unit_blocks(unit), :].rearrange("p s r -> p (s r)"),
+                x_scales[:, unit_blocks(unit), :].rearrange("p s r -> p (s r)"),
+            )
+
+        def project(acc, block, names):
+            passes = [(block + side, operand(side, name)) for side in (LEFT, RIGHT) for name in names]
+            for n, (x_block, w) in enumerate(passes):
+                nc.tensor.matmul_mx(
+                    out=acc,
+                    lhsT=x_codes[:, x_block, :].bitcast(FP8X4),
+                    lhsT_scale=x_scales[:, x_block, :],
+                    rhs=w_codes[:, w, :].bitcast(FP8X4),
+                    rhs_scale=w_scales[:, w, :],
+                    start=(n == 0),
+                    stop=(n == len(passes) - 1),
+                )
+
+        def new_bank():
+            return psum.tile([P, PAIR_COLS], F32, name="bank", tag="bank", bufs=6)
+
+        def project_pair(pair, names):
+            bank = new_bank()
+            for half in range(2):
+                project(bank[:, half * H : (half + 1) * H], 2 * pair + half, names)
+            return bank
+
+        def pair_of(blocks, pair, shift):
+            return blocks[:, 2 * pair + shift : 2 * pair + shift + 2, :].rearrange("p s h -> p (s h)")
+
+        d_bank, c_bank, lr_bank = {}, {}, {}
+        share, centre = {}, {}
+        logit, gate, mix, diff = {}, {}, {}, {}
+
+        def tensor_first(pair):
+            d_bank[pair] = project_pair(pair, ("g0", "neg_g1"))
+            c_bank[pair] = project_pair(pair, ("centre",))
+            lr_bank[pair] = new_bank()
+            nc.tensor.matmul(out=lr_bank[pair][:], lhsT=ident[:], rhs=pair_of(mix_in, pair, 0), start=True, stop=False)
+            nc.tensor.matmul(out=lr_bank[pair][:], lhsT=neg_ident[:], rhs=pair_of(mix_in, pair, 1), start=False, stop=True)
+
+        def scalar_first(pair):
+            share[pair] = stage.tile([P, PAIR_COLS], F32, name="share", tag="share")
+            nc.scalar.activation(out=share[pair][:], in_=d_bank[pair][:], func=AF.Sigmoid)
+            logit[pair] = keep.tile([P, PAIR_COLS], F32, name="logit", tag="logit")
+            nc.scalar.activation(out=logit[pair][:], in_=d_bank[pair][:], func=AF.Relu)
+            centre[pair] = stage.tile([P, PAIR_COLS], F32, name="centre", tag="centre")
+            nc.scalar.activation(out=centre[pair][:], in_=c_bank[pair][:], func=AF.Sigmoid)
+            gate[pair] = keep.tile([P, PAIR_COLS], F32, name="gate", tag="gate")
+            nc.scalar.activation(out=gate[pair][:], in_=share[pair][:], func=AF.Abs, bias=minus_half[:])
+
+        def weigh_left(pair):
+            mix[pair] = keep.tile([P, PAIR_COLS], F32, name="mix", tag="mix")
+            nc.vector.tensor_tensor(out=mix[pair][:], in0=share[pair][:], in1=lr_bank[pair][:], op=ALU.mult)
+
+        def add_right(pair):
+            nc.vector.tensor_tensor(out=mix[pair][:], in0=mix[pair][:], in1=pair_of(mix_in, pair, 1), op=ALU.add)
+
+        def subtract_mix(pair):
+            diff[pair] = keep.tile([P, PAIR_COLS], F32, name="diff", tag="diff")
+            nc.vector.tensor_tensor(out=diff[pair][:], in0=centre[pair][:], in1=mix[pair][:], op=ALU.subtract)
+
+        def logarithm(pair):
+            nc.scalar.activation(out=gate[pair][:], in_=gate[pair][:], func=AF.Ln, bias=plus_half[:])
+
+        def add_b(pair):
+            b_bank = project_pair(pair, ("g1", "neg_g2"))
+            nc.vector.tensor_tensor(out=logit[pair][:], in0=logit[pair][:], in1=b_bank[:], op=ALU.add)
+
+        def subtract_log(pair):
+            nc.vector.tensor_tensor(out=logit[pair][:], in0=logit[pair][:], in1=gate[pair][:], op=ALU.subtract)
+
+        def centre_weight(pair):
+            nc.scalar.activation(out=gate[pair][:], in_=logit[pair][:], func=AF.Sigmoid, scale=-1.0)
+
+        def weigh_centre(pair):
+            nc.vector.tensor_tensor(out=diff[pair][:], in0=diff[pair][:], in1=gate[pair][:], op=ALU.mult)
+
+        def finish(pair):
+            nc.vector.tensor_tensor(out=diff[pair][:], in0=diff[pair][:], in1=mix[pair][:], op=ALU.add)
+            nc.sync.dma_start(
+                out=out_rows[:, 2 * pair : 2 * pair + 2, :],
+                in_=diff[pair][:].rearrange("p (s h) -> p s h", s=2),
+            )
+
+        def one_behind(first, lead, follow):
+            for n in range(ROUND + 1):
+                if n < ROUND:
+                    lead(first + n)
+                if n >= 1:
+                    follow(first + n - 1)
+
+        for side in (LEFT, RIGHT):
+            prepare_weight(side, "g0")
+            prepare_weight(side, "g1")
+        spread_unit(0)
+        spread_unit(1)
+        quantise_unit(0)
+        quantise_unit(1)
+        for side in (LEFT, RIGHT):
+            prepare_weight(side, "centre")
+        spread_unit(2)
+        spread_unit(3)
+        quantise_unit(2)
+
+        tensor_first(0)
+        for pair in range(PAIRS):
+            old = pair - ROUND
+            if pair + 1 < PAIRS:
+                tensor_first(pair + 1)
+            if old >= 0:
+                centre_weight(old)
+            scalar_first(pair)
+            weigh_left(pair)
+            if pair + 3 < UNITS:
+                quantise_unit(pair + 3)
+            if old >= 0:
+                weigh_centre(old)
+            add_right(pair)
+            if pair + 4 < UNITS:
+                spread_unit(pair + 4)
+            if old >= 0:
+                finish(old)
+            subtract_mix(pair)
+            if pair in (LEFT, RIGHT):
+                prepare_weight(pair, "g2")
+            if (pair + 1) % ROUND == 0:
+                first = pair + 1 - ROUND
+                for done in range(first, pair + 1):
+                    logarithm(done)
+                one_behind(first, add_b, subtract_log)
+        for pair in range(PAIRS - ROUND, PAIRS):
+            centre_weight(pair)
+        one_behind(PAIRS - ROUND, weigh_centre, finish)

@@ -16,11 +16,19 @@ K = 512
 H = 256
 POSITIONS = 32
 BLOCKS = POSITIONS + 1
-PAIRS = POSITIONS // 2
 PAIR_COLS = 2 * H
-UNITS = (BLOCKS + 1) // 2
-ROUND = 8
-LOAD_BLOCKS = 4
+PAIRS = POSITIONS // 2
+GROUP_PAIRS = 2
+GROUP_POSITIONS = 2 * GROUP_PAIRS
+GROUP_COLS = GROUP_PAIRS * PAIR_COLS
+GROUPS = PAIRS // GROUP_PAIRS
+ROUND = 4
+PIECE_BLOCKS = 2
+UNIT_BLOCKS = GROUP_POSITIONS
+UNITS = GROUPS + 1
+LEAD = 3
+FLOOR = 40.0
+PSUM_BANKS = 8
 
 LEFT, RIGHT = 0, 1
 OPERANDS = ("centre", "g0", "g1", "neg_g1", "neg_g2")
@@ -46,12 +54,12 @@ def tile_grconv_pa_t_kernel(tc, x, x_mix, WL, WR, GL, GR, out):
         keep = ctx.enter_context(tc.tile_pool(name="keep", bufs=ROUND + 1))
         psum = ctx.enter_context(tc.psum_pool(name="psum", bufs=1))
 
-        plus_half = const.tile([P, 1], F32)
-        nc.vector.memset(plus_half[:], 0.5)
-        minus_half = const.tile([P, 1], F32)
-        nc.vector.memset(minus_half[:], -0.5)
+        plus_floor = const.tile([P, 1], F32)
+        nc.vector.memset(plus_floor[:], FLOOR)
+        minus_floor = const.tile([P, 1], F32)
+        nc.vector.memset(minus_floor[:], -FLOOR)
         warm = const.tile([P, 1], F32)
-        nc.scalar.activation(out=warm[:], in_=plus_half[:], func=AF.Sigmoid)
+        nc.scalar.activation(out=warm[:], in_=plus_floor[:], func=AF.Sigmoid)
         ident_words = const.tile([P, P], F32)
         make_identity(nc, ident_words[:])
         ident = const.tile([P, P], BF16)
@@ -70,6 +78,9 @@ def tile_grconv_pa_t_kernel(tc, x, x_mix, WL, WR, GL, GR, out):
         def operand(side, name):
             return side * len(OPERANDS) + OPERANDS.index(name)
 
+        def unit_span(unit):
+            return max(0, (unit - 1) * UNIT_BLOCKS + 1), unit * UNIT_BLOCKS + 1
+
         def load_weight(side, chunk):
             if chunk == "centre":
                 rows = centres[side]
@@ -78,28 +89,35 @@ def tile_grconv_pa_t_kernel(tc, x, x_mix, WL, WR, GL, GR, out):
             w_nat[(side, chunk)] = resident.tile([P, H // P, K], BF16, name="w_nat_%d_%s" % (side, chunk))
             nc.sync.dma_start(out=w_nat[(side, chunk)][:], in_=rows.rearrange("(t p) k -> p t k", p=P))
 
-        def load_blocks(first):
-            last = min(first + LOAD_BLOCKS, BLOCKS)
-            nc.sync.dma_start(out=x_nat[:, first:last, :], in_=x_rows[:, first:last, :])
-            nc.sync.dma_start(out=mix_in[:, first:last, :], in_=mix_rows[:, first:last, :])
+        def load_x(unit):
+            first, end = unit_span(unit)
+            nc.sync.dma_start(out=x_nat[:, first:end, :], in_=x_rows[:, first:end, :])
 
-        for side in (LEFT, RIGHT):
-            load_weight(side, "g0")
-            load_weight(side, "g1")
-        load_blocks(0)
+        def load_mix(unit):
+            first, end = unit_span(unit)
+            nc.sync.dma_start(out=mix_in[:, first:end, :], in_=mix_rows[:, first:end, :])
+
+        for chunk in ("g1", "g0"):
+            for side in (LEFT, RIGHT):
+                load_weight(side, chunk)
+        load_x(0)
+        load_x(1)
         for side in (LEFT, RIGHT):
             load_weight(side, "centre")
-        load_blocks(LOAD_BLOCKS)
+        load_mix(0)
+        load_mix(1)
+        load_x(2)
+        load_mix(2)
         for side in (LEFT, RIGHT):
             load_weight(side, "g2")
-        for first in range(2 * LOAD_BLOCKS, BLOCKS, LOAD_BLOCKS):
-            load_blocks(first)
+        for unit in range(LEAD, UNITS):
+            load_x(unit)
+            load_mix(unit)
 
-        def spread(nat, copy):
+        def transpose_words(nat):
             tiles = nat.shape[1]
-            rows = tiles * P
             nat_words = nat.bitcast(F32)
-            words = psum.tile([P, 2, rows], F32, tag="words", bufs=2)
+            words = psum.tile([P, 2, tiles * P], F32, tag="bank", bufs=PSUM_BANKS)
             for u in range(2):
                 for t in range(tiles):
                     nc.tensor.transpose(
@@ -107,21 +125,21 @@ def tile_grconv_pa_t_kernel(tc, x, x_mix, WL, WR, GL, GR, out):
                         in_=nat_words[:, t, u * P : (u + 1) * P],
                         identity=ident_words[:],
                     )
-            grouped = stage.tile([P, 4 * rows], BF16, tag="grouped", align_bytes=64)
+            return words
+
+        def copy_words(copy, words, grouped):
             copy(
-                out=grouped[:].bitcast(F32).rearrange("p (r u) -> p r u", u=2),
+                out=grouped.bitcast(F32).rearrange("p (r u) -> p r u", u=2),
                 in_=words[:].rearrange("p u r -> p r u"),
             )
-            return grouped
 
         def quantise(values, codes, scales):
             nc.vector.quantize_mx(out=codes.bitcast(FP8X4), scales=scales, in_=values)
 
-        def copy_engine(n):
-            return nc.scalar.copy if n % 2 == 0 else nc.vector.tensor_copy
-
         def prepare_weight(side, chunk):
-            grouped = spread(w_nat[(side, chunk)][:], copy_engine(side))
+            words = transpose_words(w_nat[(side, chunk)][:])
+            grouped = stage.tile([P, 4 * H], BF16, tag="w_grouped", align_bytes=64)
+            copy_words(nc.scalar.copy if side == LEFT else nc.vector.tensor_copy, words, grouped[:])
             plain, negated = CHUNK_USES[chunk]
             if plain is not None:
                 w = operand(side, plain)
@@ -132,19 +150,27 @@ def tile_grconv_pa_t_kernel(tc, x, x_mix, WL, WR, GL, GR, out):
                 nc.vector.tensor_scalar_mul(out=turned[:], in0=grouped[:], scalar1=-1.0)
                 quantise(turned[:], w_codes[:, w, :], w_scales[:, w, :])
 
-        x_grouped = {}
+        x_words, x_grouped = {}, {}
 
-        def unit_blocks(unit):
-            return slice(2 * unit, min(2 * unit + 2, BLOCKS))
+        def unit_pieces(unit):
+            first, end = unit_span(unit)
+            return [(at, min(at + PIECE_BLOCKS, end)) for at in range(first, end, PIECE_BLOCKS)]
 
-        def spread_unit(unit):
-            x_grouped[unit] = spread(x_nat[:, unit_blocks(unit), :], copy_engine(unit))
+        def transpose_unit(unit):
+            x_words[unit] = [transpose_words(x_nat[:, at:to, :]) for at, to in unit_pieces(unit)]
+
+        def copy_unit(unit):
+            first, end = unit_span(unit)
+            x_grouped[unit] = stage.tile([P, 4 * P * (end - first)], BF16, name="x_grouped", tag="x_grouped", align_bytes=64)
+            for (at, to), words in zip(unit_pieces(unit), x_words[unit]):
+                copy_words(nc.scalar.copy, words, x_grouped[unit][:, 4 * P * (at - first) : 4 * P * (to - first)])
 
         def quantise_unit(unit):
+            first, end = unit_span(unit)
             quantise(
                 x_grouped[unit][:],
-                x_codes[:, unit_blocks(unit), :].rearrange("p s r -> p (s r)"),
-                x_scales[:, unit_blocks(unit), :].rearrange("p s r -> p (s r)"),
+                x_codes[:, first:end, :].rearrange("p s r -> p (s r)"),
+                x_scales[:, first:end, :].rearrange("p s r -> p (s r)"),
             )
 
         def project(acc, block, names):
@@ -161,7 +187,7 @@ def tile_grconv_pa_t_kernel(tc, x, x_mix, WL, WR, GL, GR, out):
                 )
 
         def new_bank():
-            return psum.tile([P, PAIR_COLS], F32, name="bank", tag="bank", bufs=6)
+            return psum.tile([P, PAIR_COLS], F32, name="bank", tag="bank", bufs=PSUM_BANKS)
 
         def project_pair(pair, names):
             bank = new_bank()
@@ -169,62 +195,69 @@ def tile_grconv_pa_t_kernel(tc, x, x_mix, WL, WR, GL, GR, out):
                 project(bank[:, half * H : (half + 1) * H], 2 * pair + half, names)
             return bank
 
-        def pair_of(blocks, pair, shift):
-            return blocks[:, 2 * pair + shift : 2 * pair + shift + 2, :].rearrange("p s h -> p (s h)")
+        def mixed(first, count):
+            return mix_in[:, first : first + count, :].rearrange("p s h -> p (s h)")
+
+        def part(tiles, pair):
+            at = (pair % GROUP_PAIRS) * PAIR_COLS
+            return tiles[pair // GROUP_PAIRS][:, at : at + PAIR_COLS]
 
         d_bank, c_bank, lr_bank = {}, {}, {}
-        share, centre = {}, {}
-        logit, gate, mix, diff = {}, {}, {}, {}
+        centre = {}
+        share, logit, mix, diff = {}, {}, {}, {}
+
+        def open_group(group):
+            centre[group] = stage.tile([P, GROUP_COLS], F32, name="centre", tag="centre")
+            share[group] = keep.tile([P, GROUP_COLS], F32, name="share", tag="share")
+            logit[group] = keep.tile([P, GROUP_COLS], F32, name="logit", tag="logit")
+            mix[group] = keep.tile([P, GROUP_COLS], F32, name="mix", tag="mix")
+            diff[group] = keep.tile([P, GROUP_COLS], F32, name="diff", tag="diff")
 
         def tensor_first(pair):
             d_bank[pair] = project_pair(pair, ("g0", "neg_g1"))
             c_bank[pair] = project_pair(pair, ("centre",))
             lr_bank[pair] = new_bank()
-            nc.tensor.matmul(out=lr_bank[pair][:], lhsT=ident[:], rhs=pair_of(mix_in, pair, 0), start=True, stop=False)
-            nc.tensor.matmul(out=lr_bank[pair][:], lhsT=neg_ident[:], rhs=pair_of(mix_in, pair, 1), start=False, stop=True)
+            nc.tensor.matmul(out=lr_bank[pair][:], lhsT=ident[:], rhs=mixed(2 * pair, 2), start=True, stop=False)
+            nc.tensor.matmul(out=lr_bank[pair][:], lhsT=neg_ident[:], rhs=mixed(2 * pair + 1, 2), start=False, stop=True)
 
         def scalar_first(pair):
-            share[pair] = stage.tile([P, PAIR_COLS], F32, name="share", tag="share")
-            nc.scalar.activation(out=share[pair][:], in_=d_bank[pair][:], func=AF.Sigmoid)
-            logit[pair] = keep.tile([P, PAIR_COLS], F32, name="logit", tag="logit")
-            nc.scalar.activation(out=logit[pair][:], in_=d_bank[pair][:], func=AF.Relu)
-            centre[pair] = stage.tile([P, PAIR_COLS], F32, name="centre", tag="centre")
-            nc.scalar.activation(out=centre[pair][:], in_=c_bank[pair][:], func=AF.Sigmoid)
-            gate[pair] = keep.tile([P, PAIR_COLS], F32, name="gate", tag="gate")
-            nc.scalar.activation(out=gate[pair][:], in_=share[pair][:], func=AF.Abs, bias=minus_half[:])
+            nc.scalar.activation(out=part(logit, pair), in_=d_bank[pair][:], func=AF.Relu, bias=plus_floor[:])
+            nc.scalar.activation(out=part(centre, pair), in_=c_bank[pair][:], func=AF.Sigmoid)
+            nc.scalar.activation(out=part(share, pair), in_=part(logit, pair), func=AF.Sigmoid, bias=minus_floor[:])
 
         def weigh_left(pair):
-            mix[pair] = keep.tile([P, PAIR_COLS], F32, name="mix", tag="mix")
-            nc.vector.tensor_tensor(out=mix[pair][:], in0=share[pair][:], in1=lr_bank[pair][:], op=ALU.mult)
+            nc.vector.tensor_tensor(out=part(mix, pair), in0=part(share, pair), in1=lr_bank[pair][:], op=ALU.mult)
 
-        def add_right(pair):
-            nc.vector.tensor_tensor(out=mix[pair][:], in0=mix[pair][:], in1=pair_of(mix_in, pair, 1), op=ALU.add)
+        def add_right(group):
+            right = mixed(group * GROUP_POSITIONS + 1, GROUP_POSITIONS)
+            nc.vector.tensor_tensor(out=mix[group][:], in0=mix[group][:], in1=right, op=ALU.add)
 
-        def subtract_mix(pair):
-            diff[pair] = keep.tile([P, PAIR_COLS], F32, name="diff", tag="diff")
-            nc.vector.tensor_tensor(out=diff[pair][:], in0=centre[pair][:], in1=mix[pair][:], op=ALU.subtract)
+        def subtract_mix(group):
+            nc.vector.tensor_tensor(out=diff[group][:], in0=centre[group][:], in1=mix[group][:], op=ALU.subtract)
 
-        def logarithm(pair):
-            nc.scalar.activation(out=gate[pair][:], in_=gate[pair][:], func=AF.Ln, bias=plus_half[:])
+        def logarithm(group):
+            nc.scalar.activation(out=share[group][:], in_=share[group][:], func=AF.Ln)
 
-        def add_b(pair):
-            b_bank = project_pair(pair, ("g1", "neg_g2"))
-            nc.vector.tensor_tensor(out=logit[pair][:], in0=logit[pair][:], in1=b_bank[:], op=ALU.add)
+        def add_b(group):
+            for pair in range(group * GROUP_PAIRS, (group + 1) * GROUP_PAIRS):
+                b_bank = project_pair(pair, ("g1", "neg_g2"))
+                nc.vector.tensor_tensor(out=part(logit, pair), in0=part(logit, pair), in1=b_bank[:], op=ALU.add)
 
-        def subtract_log(pair):
-            nc.vector.tensor_tensor(out=logit[pair][:], in0=logit[pair][:], in1=gate[pair][:], op=ALU.subtract)
+        def subtract_log(group):
+            nc.vector.tensor_tensor(out=logit[group][:], in0=logit[group][:], in1=share[group][:], op=ALU.subtract)
 
-        def centre_weight(pair):
-            nc.scalar.activation(out=gate[pair][:], in_=logit[pair][:], func=AF.Sigmoid, scale=-1.0)
+        def centre_weight(group):
+            nc.scalar.activation(out=share[group][:], in_=logit[group][:], func=AF.Sigmoid, scale=-1.0, bias=plus_floor[:])
 
-        def weigh_centre(pair):
-            nc.vector.tensor_tensor(out=diff[pair][:], in0=diff[pair][:], in1=gate[pair][:], op=ALU.mult)
+        def weigh_centre(group):
+            nc.vector.tensor_tensor(out=diff[group][:], in0=diff[group][:], in1=share[group][:], op=ALU.mult)
 
-        def finish(pair):
-            nc.vector.tensor_tensor(out=diff[pair][:], in0=diff[pair][:], in1=mix[pair][:], op=ALU.add)
+        def finish(group):
+            nc.vector.tensor_tensor(out=diff[group][:], in0=diff[group][:], in1=mix[group][:], op=ALU.add)
+            first = group * GROUP_POSITIONS
             nc.sync.dma_start(
-                out=out_rows[:, 2 * pair : 2 * pair + 2, :],
-                in_=diff[pair][:].rearrange("p (s h) -> p s h", s=2),
+                out=out_rows[:, first : first + GROUP_POSITIONS, :],
+                in_=diff[group][:].rearrange("p (s h) -> p s h", s=GROUP_POSITIONS),
             )
 
         def one_behind(first, lead, follow):
@@ -234,45 +267,54 @@ def tile_grconv_pa_t_kernel(tc, x, x_mix, WL, WR, GL, GR, out):
                 if n >= 1:
                     follow(first + n - 1)
 
-        for side in (LEFT, RIGHT):
-            prepare_weight(side, "g0")
-            prepare_weight(side, "g1")
-        spread_unit(0)
-        spread_unit(1)
+        for chunk in ("g1", "g0"):
+            for side in (LEFT, RIGHT):
+                prepare_weight(side, chunk)
+        transpose_unit(0)
+        copy_unit(0)
+        transpose_unit(1)
+        copy_unit(1)
         quantise_unit(0)
         quantise_unit(1)
         for side in (LEFT, RIGHT):
             prepare_weight(side, "centre")
-        spread_unit(2)
-        spread_unit(3)
+        transpose_unit(2)
+        copy_unit(2)
         quantise_unit(2)
 
         tensor_first(0)
-        for pair in range(PAIRS):
-            old = pair - ROUND
-            if pair + 1 < PAIRS:
-                tensor_first(pair + 1)
+        for group in range(GROUPS):
+            old = group - ROUND
+            new_unit = group + LEAD
+            early, late = group * GROUP_PAIRS, group * GROUP_PAIRS + 1
+            open_group(group)
+            if new_unit < UNITS:
+                transpose_unit(new_unit)
+            tensor_first(late)
+            scalar_first(early)
+            weigh_left(early)
+            if new_unit < UNITS:
+                copy_unit(new_unit)
+            if late + 1 < PAIRS:
+                tensor_first(late + 1)
             if old >= 0:
                 centre_weight(old)
-            scalar_first(pair)
-            weigh_left(pair)
-            if pair + 3 < UNITS:
-                quantise_unit(pair + 3)
-            if old >= 0:
                 weigh_centre(old)
-            add_right(pair)
-            if pair + 4 < UNITS:
-                spread_unit(pair + 4)
+            scalar_first(late)
+            weigh_left(late)
+            add_right(group)
+            if new_unit < UNITS:
+                quantise_unit(new_unit)
             if old >= 0:
                 finish(old)
-            subtract_mix(pair)
-            if pair in (LEFT, RIGHT):
-                prepare_weight(pair, "g2")
-            if (pair + 1) % ROUND == 0:
-                first = pair + 1 - ROUND
-                for done in range(first, pair + 1):
+            subtract_mix(group)
+            if group in (LEFT, RIGHT):
+                prepare_weight(group, "g2")
+            if (group + 1) % ROUND == 0:
+                first = group + 1 - ROUND
+                for done in range(first, group + 1):
                     logarithm(done)
                 one_behind(first, add_b, subtract_log)
-        for pair in range(PAIRS - ROUND, PAIRS):
-            centre_weight(pair)
-        one_behind(PAIRS - ROUND, weigh_centre, finish)
+        for group in range(GROUPS - ROUND, GROUPS):
+            centre_weight(group)
+        one_behind(GROUPS - ROUND, weigh_centre, finish)

@@ -202,7 +202,7 @@ def tile_grconv_pa_t_kernel(tc, x, x_mix, WL, WR, GL, GR, out):
             at = (pair % GROUP_PAIRS) * PAIR_COLS
             return tiles[pair // GROUP_PAIRS][:, at : at + PAIR_COLS]
 
-        d_bank, c_bank, lr_bank = {}, {}, {}
+        d_bank, c_bank, left_right = {}, {}, {}
         centre = {}
         share, logit, mix, diff = {}, {}, {}, {}
 
@@ -216,9 +216,14 @@ def tile_grconv_pa_t_kernel(tc, x, x_mix, WL, WR, GL, GR, out):
         def tensor_first(pair):
             d_bank[pair] = project_pair(pair, ("g0", "neg_g1"))
             c_bank[pair] = project_pair(pair, ("centre",))
-            lr_bank[pair] = new_bank()
-            nc.tensor.matmul(out=lr_bank[pair][:], lhsT=ident[:], rhs=mixed(2 * pair, 2), start=True, stop=False)
-            nc.tensor.matmul(out=lr_bank[pair][:], lhsT=neg_ident[:], rhs=mixed(2 * pair + 1, 2), start=False, stop=True)
+            if pair // GROUP_PAIRS >= ROUND:
+                left_right[pair] = new_bank()
+                nc.tensor.matmul(out=left_right[pair][:], lhsT=ident[:], rhs=mixed(2 * pair, 2), start=True, stop=False)
+                nc.tensor.matmul(out=left_right[pair][:], lhsT=neg_ident[:], rhs=mixed(2 * pair + 1, 2), start=False, stop=True)
+
+        def subtract_right(pair):
+            left_right[pair] = stage.tile([P, PAIR_COLS], F32, name="left_right", tag="left_right")
+            nc.vector.tensor_tensor(out=left_right[pair][:], in0=mixed(2 * pair, 2), in1=mixed(2 * pair + 1, 2), op=ALU.subtract)
 
         def scalar_first(pair):
             nc.scalar.activation(out=part(logit, pair), in_=d_bank[pair][:], func=AF.Relu, bias=plus_floor[:])
@@ -226,14 +231,14 @@ def tile_grconv_pa_t_kernel(tc, x, x_mix, WL, WR, GL, GR, out):
             nc.scalar.activation(out=part(share, pair), in_=part(logit, pair), func=AF.Sigmoid, bias=minus_floor[:])
 
         def weigh_left(pair):
-            nc.vector.tensor_tensor(out=part(mix, pair), in0=part(share, pair), in1=lr_bank[pair][:], op=ALU.mult)
+            nc.vector.tensor_tensor(out=part(mix, pair), in0=part(share, pair), in1=left_right[pair][:], op=ALU.mult)
 
         def add_right(group):
             right = mixed(group * GROUP_POSITIONS + 1, GROUP_POSITIONS)
             nc.vector.tensor_tensor(out=mix[group][:], in0=mix[group][:], in1=right, op=ALU.add)
 
         def subtract_mix(group):
-            nc.vector.tensor_tensor(out=diff[group][:], in0=centre[group][:], in1=mix[group][:], op=ALU.subtract)
+            nc.gpsimd.tensor_tensor(out=diff[group][:], in0=centre[group][:], in1=mix[group][:], op=ALU.subtract)
 
         def logarithm(group):
             nc.scalar.activation(out=share[group][:], in_=share[group][:], func=AF.Ln)
@@ -291,6 +296,9 @@ def tile_grconv_pa_t_kernel(tc, x, x_mix, WL, WR, GL, GR, out):
             if new_unit < UNITS:
                 transpose_unit(new_unit)
             tensor_first(late)
+            if group < ROUND:
+                subtract_right(early)
+                subtract_right(late)
             scalar_first(early)
             weigh_left(early)
             if new_unit < UNITS:
@@ -302,9 +310,9 @@ def tile_grconv_pa_t_kernel(tc, x, x_mix, WL, WR, GL, GR, out):
                 weigh_centre(old)
             scalar_first(late)
             weigh_left(late)
-            add_right(group)
             if new_unit < UNITS:
                 quantise_unit(new_unit)
+            add_right(group)
             if old >= 0:
                 finish(old)
             subtract_mix(group)

from contextlib import ExitStack

import concourse.mybir as mybir
from concourse.masks import make_identity

F32 = mybir.dt.float32
BF16 = mybir.dt.bfloat16
U32 = mybir.dt.uint32
U8 = mybir.dt.uint8
FP8X4 = mybir.dt.float8_e4m3fn_x4
AF = mybir.ActivationFunctionType
ALU = mybir.AluOpType

P = 128
K = 512
H = 256
POSITIONS = 32
BLOCKS = POSITIONS + 1
PAIR_COLS = 2 * H
PAIRS = POSITIONS // 2
GROUP_PAIRS = 2
GROUP_POSITIONS = 2 * GROUP_PAIRS
GROUP_COLS = GROUP_PAIRS * PAIR_COLS
GROUPS = PAIRS // GROUP_PAIRS
ROUND = 4
PIECE_BLOCKS = 2
UNIT_BLOCKS = GROUP_POSITIONS
UNITS = GROUPS + 1
LEAD = 3
FLOOR = 40.0
PSUM_BANKS = 8

LEFT, RIGHT = 0, 1
OPERANDS = ("centre", "g0", "g1", "neg_g1", "neg_g2")
CHUNK_USES = {"centre": ("centre", None), "g0": ("g0", None), "g1": ("g1", "neg_g1"), "g2": (None, "neg_g2")}
GATE_CHUNK = {"g0": 0, "g1": 1, "g2": 2}

FLOPS = 2 * POSITIONS * P * (2 * K) * (4 * H)


def tile_grconv_pa_t_kernel(tc, x, x_mix, WL, WR, GL, GR, out):
    nc = tc.nc
    x_rows = x.rearrange("s a b k -> (a b) s k")
    mix_rows = x_mix.rearrange("s a b h -> (a b) s h")
    out_rows = out.rearrange("s a b h -> (a b) s h")
    centres = (WL, WR)
    gates = (GL, GR)

    with ExitStack() as ctx:
        ctx.enter_context(tc.manual_schedule())
        const = ctx.enter_context(tc.tile_pool(name="const", bufs=1))
        resident = ctx.enter_context(tc.tile_pool(name="resident", bufs=1))
        stage = ctx.enter_context(tc.tile_pool(name="stage", bufs=3))
        keep = ctx.enter_context(tc.tile_pool(name="keep", bufs=ROUND + 1))
        psum = ctx.enter_context(tc.psum_pool(name="psum", bufs=1))

        plus_floor = const.tile([P, 1], F32)
        nc.vector.memset(plus_floor[:], FLOOR)
        minus_floor = const.tile([P, 1], F32)
        nc.vector.memset(minus_floor[:], -FLOOR)
        warm = const.tile([P, 1], F32)
        nc.scalar.activation(out=warm[:], in_=plus_floor[:], func=AF.Sigmoid)
        ident_words = const.tile([P, P], F32)
        make_identity(nc, ident_words[:])
        ident = const.tile([P, P], BF16)
        make_identity(nc, ident[:])
        neg_ident = const.tile([P, P], BF16)
        nc.vector.tensor_scalar_mul(out=neg_ident[:], in0=ident[:], scalar1=-1.0)

        x_nat = resident.tile([P, BLOCKS, K], BF16)
        mix_in = resident.tile([P, BLOCKS, H], BF16)
        x_codes = resident.tile([P, BLOCKS, P], U32, align_bytes=64)
        x_scales = resident.tile([P, BLOCKS, P], U8, align_bytes=64)
        w_codes = resident.tile([P, 2 * len(OPERANDS), H], U32, align_bytes=64)
        w_scales = resident.tile([P, 2 * len(OPERANDS), H], U8, align_bytes=64)
        w_nat = {}

        def operand(side, name):
            return side * len(OPERANDS) + OPERANDS.index(name)

        def unit_span(unit):
            return max(0, (unit - 1) * UNIT_BLOCKS + 1), unit * UNIT_BLOCKS + 1

        def load_weight(side, chunk):
            if chunk == "centre":
                rows = centres[side]
            else:
                rows = gates[side][GATE_CHUNK[chunk] * H : (GATE_CHUNK[chunk] + 1) * H, :]
            w_nat[(side, chunk)] = resident.tile([P, H // P, K], BF16, name="w_nat_%d_%s" % (side, chunk))
            nc.sync.dma_start(out=w_nat[(side, chunk)][:], in_=rows.rearrange("(t p) k -> p t k", p=P))

        def load_x(unit):
            first, end = unit_span(unit)
            nc.sync.dma_start(out=x_nat[:, first:end, :], in_=x_rows[:, first:end, :])

        def load_mix(unit):
            first, end = unit_span(unit)
            nc.sync.dma_start(out=mix_in[:, first:end, :], in_=mix_rows[:, first:end, :])

        for chunk in ("g1", "g0"):
            for side in (LEFT, RIGHT):
                load_weight(side, chunk)
        load_x(0)
        load_x(1)
        for side in (LEFT, RIGHT):
            load_weight(side, "centre")
        load_mix(0)
        load_mix(1)
        load_x(2)
        load_mix(2)
        for side in (LEFT, RIGHT):
            load_weight(side, "g2")
        for unit in range(LEAD, UNITS):
            load_x(unit)
            load_mix(unit)

        def transpose_words(nat):
            tiles = nat.shape[1]
            nat_words = nat.bitcast(F32)
            words = psum.tile([P, 2, tiles * P], F32, tag="bank", bufs=PSUM_BANKS)
            for u in range(2):
                for t in range(tiles):
                    nc.tensor.transpose(
                        out=words[:, u, t * P : (t + 1) * P],
                        in_=nat_words[:, t, u * P : (u + 1) * P],
                        identity=ident_words[:],
                    )
            return words

        def copy_words(copy, words, grouped):
            copy(
                out=grouped.bitcast(F32).rearrange("p (r u) -> p r u", u=2),
                in_=words[:].rearrange("p u r -> p r u"),
            )

        def quantise(values, codes, scales):
            nc.vector.quantize_mx(out=codes.bitcast(FP8X4), scales=scales, in_=values)

        def prepare_weight(side, chunk):
            words = transpose_words(w_nat[(side, chunk)][:])
            grouped = stage.tile([P, 4 * H], BF16, tag="w_grouped", align_bytes=64)
            copy_words(nc.scalar.copy if side == LEFT else nc.vector.tensor_copy, words, grouped[:])
            plain, negated = CHUNK_USES[chunk]
            if plain is not None:
                w = operand(side, plain)
                quantise(grouped[:], w_codes[:, w, :], w_scales[:, w, :])
            if negated is not None:
                w = operand(side, negated)
                turned = stage.tile([P, 4 * H], BF16, tag="turned", align_bytes=64)
                nc.vector.tensor_scalar_mul(out=turned[:], in0=grouped[:], scalar1=-1.0)
                quantise(turned[:], w_codes[:, w, :], w_scales[:, w, :])

        x_words, x_grouped = {}, {}

        def unit_pieces(unit):
            first, end = unit_span(unit)
            return [(at, min(at + PIECE_BLOCKS, end)) for at in range(first, end, PIECE_BLOCKS)]

        def transpose_unit(unit):
            x_words[unit] = [transpose_words(x_nat[:, at:to, :]) for at, to in unit_pieces(unit)]

        def copy_unit(unit):
            first, end = unit_span(unit)
            x_grouped[unit] = stage.tile([P, 4 * P * (end - first)], BF16, name="x_grouped", tag="x_grouped", align_bytes=64)
            for (at, to), words in zip(unit_pieces(unit), x_words[unit]):
                copy_words(nc.scalar.copy, words, x_grouped[unit][:, 4 * P * (at - first) : 4 * P * (to - first)])

        def quantise_unit(unit):
            first, end = unit_span(unit)
            quantise(
                x_grouped[unit][:],
                x_codes[:, first:end, :].rearrange("p s r -> p (s r)"),
                x_scales[:, first:end, :].rearrange("p s r -> p (s r)"),
            )

        def project(acc, block, names):
            passes = [(block + side, operand(side, name)) for side in (LEFT, RIGHT) for name in names]
            for n, (x_block, w) in enumerate(passes):
                nc.tensor.matmul_mx(
                    out=acc,
                    lhsT=x_codes[:, x_block, :].bitcast(FP8X4),
                    lhsT_scale=x_scales[:, x_block, :],
                    rhs=w_codes[:, w, :].bitcast(FP8X4),
                    rhs_scale=w_scales[:, w, :],
                    start=(n == 0),
                    stop=(n == len(passes) - 1),
                )

        def new_bank():
            return psum.tile([P, PAIR_COLS], F32, name="bank", tag="bank", bufs=PSUM_BANKS)

        def project_pair(pair, names):
            bank = new_bank()
            for half in range(2):
                project(bank[:, half * H : (half + 1) * H], 2 * pair + half, names)
            return bank

        def mixed(first, count):
            return mix_in[:, first : first + count, :].rearrange("p s h -> p (s h)")

        def part(tiles, pair):
            at = (pair % GROUP_PAIRS) * PAIR_COLS
            return tiles[pair // GROUP_PAIRS][:, at : at + PAIR_COLS]

        d_bank, c_bank, left_right = {}, {}, {}
        centre = {}
        share, logit, mix, diff = {}, {}, {}, {}

        def open_group(group):
            centre[group] = stage.tile([P, GROUP_COLS], F32, name="centre", tag="centre")
            share[group] = keep.tile([P, GROUP_COLS], F32, name="share", tag="share")
            logit[group] = keep.tile([P, GROUP_COLS], F32, name="logit", tag="logit")
            mix[group] = keep.tile([P, GROUP_COLS], F32, name="mix", tag="mix")
            diff[group] = keep.tile([P, GROUP_COLS], F32, name="diff", tag="diff")

        def tensor_first(pair):
            d_bank[pair] = project_pair(pair, ("g0", "neg_g1"))
            c_bank[pair] = project_pair(pair, ("centre",))
            if pair // GROUP_PAIRS >= ROUND:
                left_right[pair] = new_bank()
                nc.tensor.matmul(out=left_right[pair][:], lhsT=ident[:], rhs=mixed(2 * pair, 2), start=True, stop=False)
                nc.tensor.matmul(out=left_right[pair][:], lhsT=neg_ident[:], rhs=mixed(2 * pair + 1, 2), start=False, stop=True)

        def subtract_right(pair):
            left_right[pair] = stage.tile([P, PAIR_COLS], F32, name="left_right", tag="left_right")
            nc.vector.tensor_tensor(out=left_right[pair][:], in0=mixed(2 * pair, 2), in1=mixed(2 * pair + 1, 2), op=ALU.subtract)

        def scalar_first(pair):
            nc.scalar.activation(out=part(logit, pair), in_=d_bank[pair][:], func=AF.Relu, bias=plus_floor[:])
            nc.scalar.activation(out=part(centre, pair), in_=c_bank[pair][:], func=AF.Sigmoid)
            nc.scalar.activation(out=part(share, pair), in_=part(logit, pair), func=AF.Sigmoid, bias=minus_floor[:])

        def weigh_left(pair):
            nc.vector.tensor_tensor(out=part(mix, pair), in0=part(share, pair), in1=left_right[pair][:], op=ALU.mult)

        def add_right(group):
            right = mixed(group * GROUP_POSITIONS + 1, GROUP_POSITIONS)
            nc.vector.tensor_tensor(out=mix[group][:], in0=mix[group][:], in1=right, op=ALU.add)

        def subtract_mix(group):
            nc.gpsimd.tensor_tensor(out=diff[group][:], in0=centre[group][:], in1=mix[group][:], op=ALU.subtract)

        def logarithm(group):
            nc.scalar.activation(out=share[group][:], in_=share[group][:], func=AF.Ln)

        def add_b(group):
            for pair in range(group * GROUP_PAIRS, (group + 1) * GROUP_PAIRS):
                b_bank = project_pair(pair, ("g1", "neg_g2"))
                nc.vector.tensor_tensor(out=part(logit, pair), in0=part(logit, pair), in1=b_bank[:], op=ALU.add)

        def subtract_log(group):
            nc.vector.tensor_tensor(out=logit[group][:], in0=logit[group][:], in1=share[group][:], op=ALU.subtract)

        def centre_weight(group):
            nc.scalar.activation(out=share[group][:], in_=logit[group][:], func=AF.Sigmoid, scale=-1.0, bias=plus_floor[:])

        def weigh_centre(group):
            nc.vector.tensor_tensor(out=diff[group][:], in0=diff[group][:], in1=share[group][:], op=ALU.mult)

        def finish(group):
            nc.vector.tensor_tensor(out=diff[group][:], in0=diff[group][:], in1=mix[group][:], op=ALU.add)
            first = group * GROUP_POSITIONS
            nc.sync.dma_start(
                out=out_rows[:, first : first + GROUP_POSITIONS, :],
                in_=diff[group][:].rearrange("p (s h) -> p s h", s=GROUP_POSITIONS),
            )

        def one_behind(first, lead, follow):
            for n in range(ROUND + 1):
                if n < ROUND:
                    lead(first + n)
                if n >= 1:
                    follow(first + n - 1)

        for chunk in ("g1", "g0"):
            for side in (LEFT, RIGHT):
                prepare_weight(side, chunk)
        transpose_unit(0)
        copy_unit(0)
        transpose_unit(1)
        copy_unit(1)
        quantise_unit(0)
        quantise_unit(1)
        for side in (LEFT, RIGHT):
            prepare_weight(side, "centre")
        transpose_unit(2)
        copy_unit(2)
        quantise_unit(2)

        tensor_first(0)
        for group in range(GROUPS):
            old = group - ROUND
            new_unit = group + LEAD
            early, late = group * GROUP_PAIRS, group * GROUP_PAIRS + 1
            open_group(group)
            if new_unit < UNITS:
                transpose_unit(new_unit)
            tensor_first(late)
            if group < ROUND:
                subtract_right(early)
                subtract_right(late)
            scalar_first(early)
            weigh_left(early)
            if new_unit < UNITS:
                copy_unit(new_unit)
            if late + 1 < PAIRS:
                tensor_first(late + 1)
            if old >= 0:
                centre_weight(old)
                weigh_centre(old)
            scalar_first(late)
            weigh_left(late)
            if new_unit < UNITS:
                quantise_unit(new_unit)
            add_right(group)
            if old >= 0:
                finish(old)
            subtract_mix(group)
            if group in (LEFT, RIGHT):
                prepare_weight(group, "g2")
            if (group + 1) % ROUND == 0:
                first = group + 1 - ROUND
                for done in range(first, group + 1):
                    logarithm(done)
                one_behind(first, add_b, subtract_log)
        for group in range(GROUPS - ROUND, GROUPS):
            centre_weight(group)
        one_behind(GROUPS - ROUND, weigh_centre, finish)
